import numpy as np
import ml_dtypes


def mxq(x, axis, fmt="e4m3"):
    dtype, down = {"e4m3": (ml_dtypes.float8_e4m3fn, 7), "e5m2": (ml_dtypes.float8_e5m2, 14)}[fmt]
    v = np.moveaxis(np.asarray(x, np.float32).astype(ml_dtypes.bfloat16).astype(np.float64), axis, -1)
    blocks = v.reshape(v.shape[:-1] + (-1, 32))
    amax = np.abs(blocks).max(-1, keepdims=True)
    byte = np.maximum(np.where(amax > 0, np.frexp(amax)[1] - 1 + 127, 0) - down, 1)
    scale = np.exp2(byte - 127.0)
    codes = (blocks / scale).astype(np.float32).astype(dtype).astype(np.float64)
    return np.moveaxis((codes * scale).reshape(v.shape), -1, axis)


WIDE = False


def mx_kscale(k):
    if not WIDE:
        return np.ones(k)
    levels = np.array([10, -10, 5, -5, 0])
    if k % 512:
        return np.exp2(np.random.permutation(np.resize(levels, k // 32))).repeat(32)
    a = np.empty((k // 512, 16))
    for p in range(k // 512):
        a[p, :8] = np.random.permutation(np.resize(levels, 8))
        for g in range(8):
            far = levels[np.abs(levels - a[p, g]) >= 10]
            a[p, g + 8] = far[np.random.randint(len(far))]
    return np.exp2(a.ravel()).repeat(32)


BF16 = ml_dtypes.bfloat16


def bf(x):
    return np.asarray(x, np.float32).astype(BF16)


def f64(x):
    return np.asarray(x).astype(np.float64)


N, D, H, E = 1024, 512, 2048, 8

CLAMP_MAX = float(np.log(100.0))


def setup_inputs():
    s, t = mx_kscale(D), mx_kscale(H)
    return {"x": bf(np.random.standard_normal((N, D)) * s),
            "W1": bf(np.random.standard_normal((E, D, H)) / np.sqrt(D) / s[:, None] * t),
            "b1": bf(np.random.standard_normal((E, H)) * 0.1 * t),
            "W2": bf(np.random.standard_normal((E, H, D)) / np.sqrt(H) / t[:, None]),
            "b2": bf(np.random.standard_normal((E, D)) * 0.1),
            "temperature": bf(np.log(2.0) + 0.1 * np.random.standard_normal((1,)))}


def reference(x, W1, b1, W2, b2, temperature):
    xe = f64(x).reshape(E, N // E, D)
    h = np.maximum(f64(bf(mxq(xe, 2, "e4m3") @ mxq(f64(W1), 1, "e4m3"))) + f64(b1)[:, None, :], 0.0)
    y = (mxq(h, 2, "e4m3") @ mxq(f64(W2), 1, "e4m3")) + f64(b2)[:, None, :]
    logit_scale = np.exp(np.minimum(f64(temperature), CLAMP_MAX))
    return y.reshape(N, D) * logit_scale

@@ -1,0 +1,292 @@
+from contextlib import ExitStack
+import math
+
+import concourse.mybir as mybir
+from concourse.masks import make_identity
+
+N_TOK, D, H, E = 1024, 512, 2048, 8
+FLOPS = 4 * N_TOK * D * H
+
+F32 = mybir.dt.float32
+BF16 = mybir.dt.bfloat16
+U32 = mybir.dt.uint32
+U8 = mybir.dt.uint8
+FP8X4 = mybir.dt.float8_e4m3fn_x4
+ALU = mybir.AluOpType
+ACT = mybir.ActivationFunctionType
+
+P = 128
+PACK = 4
+N_TILE = 512
+UNITS = 4
+CLAMP_MAX = math.log(100.0)
+
+RAW_BUFS = 7
+SCALAR_UNITS = 35
+SCALAR_LEAD = 3
+VECTOR_LEAD = 1
+X_TURN = 6
+X_COPY = 4
+X_QUANT = 1
+BANK_LAG = 2
+BIAS_LAG = 4
+M2_LAG = 2
+FAST = True
+EARLY = 3
+
+
+def tile_moelayer_kernel(tc, x, W1, b1, W2, b2, temperature, out):
+    nc = tc.nc
+
+    stream = [(1, 0, q) for q in range(UNITS)]
+    for e in range(1, E):
+        stream.extend([(1, e, q) for q in range(UNITS)])
+        stream.extend([(2, e - 1, q) for q in range(UNITS)])
+    stream.extend([(2, E - 1, q) for q in range(UNITS)])
+    n_units = len(stream)
+
+    def unit(n):
+        return stream[n] if 0 <= n < n_units else (0, 0, 0)
+
+    def on_scalar(n):
+        return ((n + 1) * SCALAR_UNITS) // n_units > (n * SCALAR_UNITS) // n_units
+
+    with ExitStack() as ctx:
+        const = ctx.enter_context(tc.tile_pool(name="const", bufs=1))
+        work = ctx.enter_context(tc.tile_pool(name="work", bufs=2))
+        psum = ctx.enter_context(tc.psum_pool(name="psum", bufs=8))
+        ctx.enter_context(tc.manual_schedule())
+
+        raw_unit = {}
+        grouped = {}
+        codes = {}
+        scales = {}
+        bank = {}
+        turned = {}
+        h_rows = {}
+        x_rows = {}
+        x_turned = {}
+        x_grouped = {}
+        x_codes = {}
+        x_scales = {}
+        h_biased = {}
+        h_relu = {}
+        h_codes = {}
+        h_scales = {}
+        acc = {}
+        b2_rows = {}
+        b2_scaled = {}
+
+        def load_matrix(w):
+            kind, e, q0 = stream[UNITS * w]
+            if kind == 1:
+                x_rows[e] = work.tile([P, D], BF16, tag="x_rows", name="x_rows", bufs=E)
+                queue = nc.scalar if w == 0 else nc.sync
+                queue.dma_start(out=x_rows[e][:], in_=x[e * P : (e + 1) * P, :])
+                raw = work.tile([P, PACK, H], BF16, tag="raw", name="raw", bufs=RAW_BUFS)
+                src = W1[e].rearrange("(p j) h -> p j h", j=PACK)
+                pieces = UNITS if w < EARLY else 1
+                width = H // pieces
+                for c in range(pieces):
+                    cols = slice(c * width, (c + 1) * width)
+                    nc.sync.dma_start(out=raw[:, :, cols], in_=src[:, :, cols])
+                for q in range(UNITS):
+                    raw_unit[UNITS * w + q] = raw[:, :, q * N_TILE : (q + 1) * N_TILE]
+            else:
+                b2_rows[e] = work.tile([P, D], BF16, tag="b2_rows", name="b2_rows", bufs=E)
+                nc.sync.dma_start(out=b2_rows[e][:], in_=b2[e].partition_broadcast(P))
+                raw = work.tile([P, UNITS, PACK, D], BF16, tag="raw", name="raw", bufs=RAW_BUFS)
+                src = W2[e].rearrange("(g p j) d -> p g j d", g=UNITS, j=PACK)
+                pieces = UNITS if w < EARLY else 1
+                width = UNITS // pieces
+                for c in range(pieces):
+                    rows = slice(c * width, (c + 1) * width)
+                    nc.sync.dma_start(out=raw[:, rows], in_=src[:, rows])
+                for q in range(UNITS):
+                    raw_unit[UNITS * w + q] = raw[:, q]
+
+        def interleave(n):
+            g = work.tile([P, N_TILE, PACK], BF16, tag="grouped", name="grouped", bufs=6, align_bytes=64)
+            grouped[n] = g
+            if FAST:
+                dst = g.rearrange("p (c i) j -> p c j i", i=4)
+                src = raw_unit[n].rearrange("p j (c i) -> p c j i", i=4)
+            else:
+                dst = g[:]
+                src = raw_unit[n].rearrange("p j c -> p c j")
+            if on_scalar(n):
+                nc.scalar.copy(out=dst, in_=src)
+            else:
+                nc.vector.tensor_copy(out=dst, in_=src)
+
+        def quantize(n):
+            codes[n] = work.tile([P, N_TILE], U32, tag="codes", name="codes", bufs=6, align_bytes=64)
+            scales[n] = work.tile([P, N_TILE], U8, tag="scales", name="scales", bufs=6, align_bytes=64)
+            nc.vector.quantize_mx(
+                out=codes[n][:].bitcast(FP8X4),
+                scales=scales[n][:],
+                in_=grouped[n].rearrange("p c j -> p (c j)"),
+            )
+
+        def multiply(n):
+            kind, e, q = stream[n]
+            if kind == 1:
+                bank[n] = psum.tile([P, N_TILE], BF16, tag="bank", name="bank")
+                nc.tensor.matmul_mx(
+                    out=bank[n][:],
+                    lhsT=x_codes[e][:].bitcast(FP8X4),
+                    lhsT_scale=x_scales[e][:],
+                    rhs=codes[n][:].bitcast(FP8X4),
+                    rhs_scale=scales[n][:],
+                    start=True,
+                    stop=True,
+                )
+            else:
+                if q == 0:
+                    acc[e] = psum.tile([P, D], F32, tag="bank", name="acc")
+                nc.tensor.matmul_mx(
+                    out=acc[e][:],
+                    lhsT=h_codes[e][:, q, :].bitcast(FP8X4),
+                    lhsT_scale=h_scales[e][:, q, :],
+                    rhs=codes[n][:].bitcast(FP8X4),
+                    rhs_scale=scales[n][:],
+                    start=(q == 0),
+                    stop=(q == UNITS - 1),
+                )
+
+        def empty_bank(n):
+            h_rows[n] = work.tile([P, N_TILE], BF16, tag="h_rows", name="h_rows", bufs=3)
+            nc.scalar.copy(out=h_rows[n][:], in_=bank[n][:])
+
+        def turn(n):
+            turned[n] = turn_words(h_rows[n])
+
+        def add_bias(n):
+            kind, e, q = stream[n]
+            if q == 0:
+                h_biased[e] = work.tile([P, UNITS, P, PACK], BF16, tag="h_biased", name="h_biased", bufs=2)
+            row = UNITS * e + q
+            nc.vector.tensor_tensor(
+                out=h_biased[e][:, q].rearrange("p r (u w) -> p r u w", w=2),
+                in0=turned[n][:].bitcast(BF16).rearrange("p u (r w) -> p r u w", w=2),
+                in1=b1_grouped[:, row : row + 1, :].to_broadcast([P, P, PACK]).rearrange("p r (u w) -> p r u w", w=2),
+                op=ALU.add,
+            )
+
+        def relu(e):
+            h_relu[e] = work.tile([P, UNITS, P, PACK], BF16, tag="h_relu", name="h_relu", bufs=2, align_bytes=64)
+            nc.vector.tensor_scalar_max(
+                out=h_relu[e].rearrange("p q r t -> p (q r t)"),
+                in0=h_biased[e].rearrange("p q r t -> p (q r t)"),
+                scalar1=0.0,
+            )
+
+        def quantize_h(e):
+            h_codes[e] = work.tile([P, UNITS, P], U32, tag="h_codes", name="h_codes", bufs=2, align_bytes=64)
+            h_scales[e] = work.tile([P, UNITS, P], U8, tag="h_scales", name="h_scales", bufs=2, align_bytes=64)
+            nc.vector.quantize_mx(
+                out=h_codes[e].rearrange("p q r -> p (q r)").bitcast(FP8X4),
+                scales=h_scales[e].rearrange("p q r -> p (q r)"),
+                in_=h_relu[e].rearrange("p q r t -> p (q r t)"),
+            )
+
+        def scale_b2(e):
+            b2_scaled[e] = work.tile([P, D], F32, tag="b2_scaled", name="b2_scaled", bufs=2)
+            nc.scalar.activation(out=b2_scaled[e][:], in_=b2_rows[e][:], func=ACT.Copy, scale=logit_scale[:, 0:1])
+
+        def finish(e):
+            res = work.tile([P, D], F32, tag="res", name="res", bufs=2)
+            nc.vector.scalar_tensor_tensor(
+                out=res[:],
+                in0=acc[e][:],
+                scalar=logit_scale[:, 0:1],
+                in1=b2_scaled[e][:],
+                op0=ALU.mult,
+                op1=ALU.add,
+            )
+            nc.sync.dma_start(out=out[e * P : (e + 1) * P, :], in_=res[:])
+
+        def turn_words(rows):
+            words = rows[:].bitcast(F32)
+            t = psum.tile([P, 2, P], F32, tag="bank", name="words")
+            for u in range(2):
+                nc.tensor.transpose(out=t[:, u, :], in_=words[:, u::2], identity=ident[:])
+            return t
+
+        def quantize_x(e):
+            x_codes[e] = work.tile([P, P], U32, tag="x_codes", name="x_codes", bufs=2, align_bytes=64)
+            x_scales[e] = work.tile([P, P], U8, tag="x_scales", name="x_scales", bufs=2, align_bytes=64)
+            nc.vector.quantize_mx(
+                out=x_codes[e][:].bitcast(FP8X4),
+                scales=x_scales[e][:],
+                in_=x_grouped[e].rearrange("p r t -> p (r t)"),
+            )
+
+        zero = const.tile([P, 1], F32, tag="zero", name="zero")
+        warm = const.tile([P, 1], F32, tag="warm", name="warm")
+        temp = const.tile([P, 1], BF16, tag="temp", name="temp")
+        clamped = const.tile([P, 1], F32, tag="clamped", name="clamped")
+        logit_scale = const.tile([P, 1], F32, tag="logit_scale", name="logit_scale")
+        ident = const.tile([P, P], F32, tag="ident", name="ident")
+        b1_rows = const.tile([P, D], BF16, tag="b1_rows", name="b1_rows")
+        b1_grouped = const.tile([P, P, PACK], BF16, tag="b1_grouped", name="b1_grouped")
+
+        nc.gpsimd.memset(zero[:], 0.0)
+        nc.gpsimd.memset(b1_rows[:], 0.0)
+        make_identity(nc, ident[:])
+        for w in range(RAW_BUFS):
+            load_matrix(w)
+        nc.scalar.dma_start(out=temp[:], in_=temperature.partition_broadcast(P))
+        nc.scalar.activation(out=warm[:], in_=zero[:], func=ACT.Exp)
+        nc.scalar.dma_start(out=b1_rows[0 : E * UNITS, :], in_=b1.rearrange("e (q c) -> (e q) c", q=UNITS))
+
+        b1_turned = {}
+        for s in range(-X_TURN, n_units + M2_LAG + 2):
+            if unit(s - BANK_LAG)[0] == 1:
+                empty_bank(s - BANK_LAG)
+            kind, e, q = unit(s + X_COPY)
+            if kind == 1 and q == 0:
+                x_grouped[e] = work.tile([P, P, PACK], BF16, tag="x_grouped", name="x_grouped", bufs=2, align_bytes=64)
+                nc.scalar.copy(out=x_grouped[e][:].bitcast(F32), in_=x_turned[e].rearrange("p u r -> p r u"))
+            if s == 2:
+                nc.scalar.activation(out=logit_scale[:], in_=clamped[:], func=ACT.Exp)
+            kind, e, q = unit(s)
+            if kind == 2 and q == 0:
+                scale_b2(e)
+            if unit(s + SCALAR_LEAD)[0] and on_scalar(s + SCALAR_LEAD):
+                interleave(s + SCALAR_LEAD)
+            if unit(s + VECTOR_LEAD)[0] and not on_scalar(s + VECTOR_LEAD):
+                interleave(s + VECTOR_LEAD)
+            if unit(s)[0]:
+                quantize(s)
+            if s == 1:
+                nc.vector.tensor_scalar_min(out=clamped[:], in0=temp[:], scalar1=CLAMP_MAX)
+            if s == 3:
+                nc.vector.tensor_copy(out=b1_grouped[:].bitcast(F32), in_=b1_turned[0].rearrange("p u r -> p r u"))
+            if unit(s - BIAS_LAG)[0] == 1:
+                add_bias(s - BIAS_LAG)
+            kind, e, q = unit(s - BIAS_LAG - 1)
+            if kind == 1 and q == UNITS - 1:
+                relu(e)
+            kind, e, q = unit(s - BIAS_LAG - 2)
+            if kind == 1 and q == UNITS - 1:
+                quantize_h(e)
+            kind, e, q = unit(s + X_QUANT)
+            if kind == 1 and q == 0:
+                quantize_x(e)
+            kind, e, q = unit(s - M2_LAG - 1)
+            if kind == 2 and q == UNITS - 1:
+                finish(e)
+            kind, e, q = unit(s + X_TURN)
+            if kind == 1 and q == 0:
+                x_turned[e] = turn_words(x_rows[e])
+            if s == 1:
+                b1_turned[0] = turn_words(b1_rows)
+            if unit(s - BANK_LAG)[0] == 1:
+                turn(s - BANK_LAG)
+            if unit(s)[0] == 1:
+                multiply(s)
+            if unit(s - M2_LAG)[0] == 2:
+                multiply(s - M2_LAG)
+            if s >= 0 and s % UNITS == UNITS - 1 and s // UNITS + RAW_BUFS < 2 * E:
+                load_matrix(s // UNITS + RAW_BUFS)

@@ -31,7 +31,9 @@ X_QUANT = 1
 BANK_LAG = 2
 BIAS_LAG = 4
 M2_LAG = 2
-FAST = True
+G_COLS = 256
+BATCH_LAG = 7
+G_AHEAD = 4
 EARLY = 3
 
 
@@ -47,6 +49,14 @@ def tile_moelayer_kernel(tc, x, W1, b1, W2, b2, temperature, out):
 
     def unit(n):
         return stream[n] if 0 <= n < n_units else (0, 0, 0)
+
+    first = [stream.index((1, e, 0)) for e in range(E)]
+    batch_steps = [first[e] + BATCH_LAG for e in range(E)]
+    finish_step = {}
+    for e in range(E):
+        ready = stream.index((2, e, UNITS - 1)) + M2_LAG + 1
+        later = [b for b in batch_steps if b >= ready]
+        finish_step[e] = min(later) if later else ready
 
     def on_scalar(n):
         return ((n + 1) * SCALAR_UNITS) // n_units > (n * SCALAR_UNITS) // n_units
@@ -105,15 +115,27 @@ def tile_moelayer_kernel(tc, x, W1, b1, W2, b2, temperature, out):
                 for q in range(UNITS):
                     raw_unit[UNITS * w + q] = raw[:, q]
 
+        def interleave_gpsimd(n):
+            grouped[n] = work.tile([P, N_TILE, PACK], BF16, tag="grouped_g", name="grouped_g", bufs=1, align_bytes=64)
+            nc.gpsimd.tensor_scalar(
+                out=grouped[n][:, 0:G_COLS, :],
+                in0=raw_unit[n][:, :, 0:G_COLS].rearrange("p j c -> p c j"),
+                scalar1=1.0,
+                scalar2=0.0,
+                op0=ALU.mult,
+                op1=ALU.add,
+            )
+
         def interleave(n):
-            g = work.tile([P, N_TILE, PACK], BF16, tag="grouped", name="grouped", bufs=6, align_bytes=64)
-            grouped[n] = g
-            if FAST:
-                dst = g.rearrange("p (c i) j -> p c j i", i=4)
-                src = raw_unit[n].rearrange("p j (c i) -> p c j i", i=4)
+            lo = 0
+            if n in grouped:
+                lo = G_COLS
+            elif n in batch_steps:
+                grouped[n] = work.tile([P, N_TILE, PACK], BF16, tag="grouped_g", name="grouped_g", bufs=1, align_bytes=64)
             else:
-                dst = g[:]
-                src = raw_unit[n].rearrange("p j c -> p c j")
+                grouped[n] = work.tile([P, N_TILE, PACK], BF16, tag="grouped", name="grouped", bufs=6, align_bytes=64)
+            dst = grouped[n][:, lo:N_TILE, :].rearrange("p (c i) j -> p c j i", i=4)
+            src = raw_unit[n][:, :, lo:N_TILE].rearrange("p j (c i) -> p c j i", i=4)
             if on_scalar(n):
                 nc.scalar.copy(out=dst, in_=src)
             else:
@@ -259,24 +281,25 @@ def tile_moelayer_kernel(tc, x, W1, b1, W2, b2, temperature, out):
                 interleave(s + VECTOR_LEAD)
             if unit(s)[0]:
                 quantize(s)
+            if s in batch_steps[1:]:
+                interleave_gpsimd(s + G_AHEAD)
             if s == 1:
                 nc.vector.tensor_scalar_min(out=clamped[:], in0=temp[:], scalar1=CLAMP_MAX)
             if s == 3:
                 nc.vector.tensor_copy(out=b1_grouped[:].bitcast(F32), in_=b1_turned[0].rearrange("p u r -> p r u"))
-            if unit(s - BIAS_LAG)[0] == 1:
-                add_bias(s - BIAS_LAG)
-            kind, e, q = unit(s - BIAS_LAG - 1)
-            if kind == 1 and q == UNITS - 1:
-                relu(e)
-            kind, e, q = unit(s - BIAS_LAG - 2)
-            if kind == 1 and q == UNITS - 1:
-                quantize_h(e)
+            if s in batch_steps:
+                for q in range(UNITS):
+                    add_bias(s - BATCH_LAG + q)
+            for e in range(E):
+                if finish_step[e] == s:
+                    finish(e)
+            if s - 1 in batch_steps:
+                relu(batch_steps.index(s - 1))
+            if s - 2 in batch_steps:
+                quantize_h(batch_steps.index(s - 2))
             kind, e, q = unit(s + X_QUANT)
             if kind == 1 and q == 0:
                 quantize_x(e)
-            kind, e, q = unit(s - M2_LAG - 1)
-            if kind == 2 and q == UNITS - 1:
-                finish(e)
             kind, e, q = unit(s + X_TURN)
             if kind == 1 and q == 0:
                 x_turned[e] = turn_words(x_rows[e])

@@ -91,7 +91,7 @@ def tile_moelayer_kernel(tc, x, W1, b1, W2, b2, temperature, out):
             kind, e, q0 = stream[UNITS * w]
             if kind == 1:
                 x_rows[e] = work.tile([P, D], BF16, tag="x_rows", name="x_rows", bufs=E)
-                queue = nc.scalar if w == 0 else nc.sync
+                queue = nc.scalar if w < 2 else nc.sync
                 queue.dma_start(out=x_rows[e][:], in_=x[e * P : (e + 1) * P, :])
                 raw = work.tile([P, PACK, H], BF16, tag="raw", name="raw", bufs=RAW_BUFS)
                 src = W1[e].rearrange("(p j) h -> p j h", j=PACK)
@@ -181,7 +181,11 @@ def tile_moelayer_kernel(tc, x, W1, b1, W2, b2, temperature, out):
             nc.scalar.copy(out=h_rows[n][:], in_=bank[n][:])
 
         def turn(n):
-            turned[n] = turn_words(h_rows[n])
+            if n % 2 == 0:
+                turned[n] = psum.tile([P, 2, 2, P], F32, tag="bank", name="turned")
+            words = h_rows[n][:].bitcast(F32)
+            for u in range(2):
+                nc.tensor.transpose(out=turned[n - n % 2][:, u, n % 2, :], in_=words[:, u::2], identity=ident[:])
 
         def add_bias(n):
             kind, e, q = stream[n]
@@ -189,9 +193,9 @@ def tile_moelayer_kernel(tc, x, W1, b1, W2, b2, temperature, out):
                 h_biased[e] = work.tile([P, UNITS, P, PACK], BF16, tag="h_biased", name="h_biased", bufs=2)
             row = UNITS * e + q
             nc.vector.tensor_tensor(
-                out=h_biased[e][:, q].rearrange("p r (u w) -> p r u w", w=2),
-                in0=turned[n][:].bitcast(BF16).rearrange("p u (r w) -> p r u w", w=2),
-                in1=b1_grouped[:, row : row + 1, :].to_broadcast([P, P, PACK]).rearrange("p r (u w) -> p r u w", w=2),
+                out=h_biased[e][:, q : q + 2].rearrange("p a r (u w) -> p a r u w", w=2),
+                in0=turned[n][:].bitcast(BF16).rearrange("p u a (r w) -> p a r u w", w=2),
+                in1=b1_grouped[:, row : row + 2, :].unsqueeze(2).to_broadcast([P, 2, P, PACK]).rearrange("p a r (u w) -> p a r u w", w=2),
                 op=ALU.add,
             )
 
@@ -288,7 +292,7 @@ def tile_moelayer_kernel(tc, x, W1, b1, W2, b2, temperature, out):
             if s == 3:
                 nc.vector.tensor_copy(out=b1_grouped[:].bitcast(F32), in_=b1_turned[0].rearrange("p u r -> p r u"))
             if s in batch_steps:
-                for q in range(UNITS):
+                for q in range(0, UNITS, 2):
                     add_bias(s - BATCH_LAG + q)
             for e in range(E):
                 if finish_step[e] == s:

@@ -35,6 +35,9 @@ G_COLS = 256
 BATCH_LAG = 7
 G_AHEAD = 4
 EARLY = 3
+BANKS = 7
+T_COLS = 64
+B2_AHEAD = 2
 
 
 def tile_moelayer_kernel(tc, x, W1, b1, W2, b2, temperature, out):
@@ -84,7 +87,7 @@ def tile_moelayer_kernel(tc, x, W1, b1, W2, b2, temperature, out):
         h_codes = {}
         h_scales = {}
         acc = {}
-        b2_rows = {}
+        b2_wide = {}
         b2_scaled = {}
 
         def load_matrix(w):
@@ -103,8 +106,6 @@ def tile_moelayer_kernel(tc, x, W1, b1, W2, b2, temperature, out):
                 for q in range(UNITS):
                     raw_unit[UNITS * w + q] = raw[:, :, q * N_TILE : (q + 1) * N_TILE]
             else:
-                b2_rows[e] = work.tile([P, D], BF16, tag="b2_rows", name="b2_rows", bufs=E)
-                nc.sync.dma_start(out=b2_rows[e][:], in_=b2[e].partition_broadcast(P))
                 raw = work.tile([P, UNITS, PACK, D], BF16, tag="raw", name="raw", bufs=RAW_BUFS)
                 src = W2[e].rearrange("(g p j) d -> p g j d", g=UNITS, j=PACK)
                 pieces = UNITS if w < EARLY else 1
@@ -153,7 +154,7 @@ def tile_moelayer_kernel(tc, x, W1, b1, W2, b2, temperature, out):
         def multiply(n):
             kind, e, q = stream[n]
             if kind == 1:
-                bank[n] = psum.tile([P, N_TILE], BF16, tag="bank", name="bank")
+                bank[n] = psum.tile([P, N_TILE], BF16, tag="bank", name="bank", bufs=BANKS)
                 nc.tensor.matmul_mx(
                     out=bank[n][:],
                     lhsT=x_codes[e][:].bitcast(FP8X4),
@@ -165,7 +166,7 @@ def tile_moelayer_kernel(tc, x, W1, b1, W2, b2, temperature, out):
                 )
             else:
                 if q == 0:
-                    acc[e] = psum.tile([P, D], F32, tag="bank", name="acc")
+                    acc[e] = psum.tile([P, D], F32, tag="bank", name="acc", bufs=BANKS)
                 nc.tensor.matmul_mx(
                     out=acc[e][:],
                     lhsT=h_codes[e][:, q, :].bitcast(FP8X4),
@@ -182,7 +183,7 @@ def tile_moelayer_kernel(tc, x, W1, b1, W2, b2, temperature, out):
 
         def turn(n):
             if n % 2 == 0:
-                turned[n] = psum.tile([P, 2, 2, P], F32, tag="bank", name="turned")
+                turned[n] = psum.tile([P, 2, 2, P], F32, tag="bank", name="turned", bufs=BANKS)
             words = h_rows[n][:].bitcast(F32)
             for u in range(2):
                 nc.tensor.transpose(out=turned[n - n % 2][:, u, n % 2, :], in_=words[:, u::2], identity=ident[:])
@@ -216,9 +217,20 @@ def tile_moelayer_kernel(tc, x, W1, b1, W2, b2, temperature, out):
                 in_=h_relu[e].rearrange("p q r t -> p (q r t)"),
             )
 
+        def spread_row(rows, r, width):
+            t = psum.tile([P, width], F32, tag="spread", name="spread", bufs=1)
+            nc.tensor.matmul(
+                out=t[:],
+                lhsT=ident_bf[:, r : r + 1].to_broadcast([P, P]),
+                rhs=rows[:, 0:width],
+                start=True,
+                stop=True,
+            )
+            return t
+
         def scale_b2(e):
             b2_scaled[e] = work.tile([P, D], F32, tag="b2_scaled", name="b2_scaled", bufs=2)
-            nc.scalar.activation(out=b2_scaled[e][:], in_=b2_rows[e][:], func=ACT.Copy, scale=logit_scale[:, 0:1])
+            nc.scalar.activation(out=b2_scaled[e][:], in_=b2_wide[e][:], func=ACT.Copy, scale=logit_scale[:, 0:1])
 
         def finish(e):
             res = work.tile([P, D], F32, tag="res", name="res", bufs=2)
@@ -234,7 +246,7 @@ def tile_moelayer_kernel(tc, x, W1, b1, W2, b2, temperature, out):
 
         def turn_words(rows):
             words = rows[:].bitcast(F32)
-            t = psum.tile([P, 2, P], F32, tag="bank", name="words")
+            t = psum.tile([P, 2, P], F32, tag="bank", name="words", bufs=BANKS)
             for u in range(2):
                 nc.tensor.transpose(out=t[:, u, :], in_=words[:, u::2], identity=ident[:])
             return t
@@ -250,7 +262,9 @@ def tile_moelayer_kernel(tc, x, W1, b1, W2, b2, temperature, out):
 
         zero = const.tile([P, 1], F32, tag="zero", name="zero")
         warm = const.tile([P, 1], F32, tag="warm", name="warm")
-        temp = const.tile([P, 1], BF16, tag="temp", name="temp")
+        temp_row = const.tile([P, T_COLS], BF16, tag="temp_row", name="temp_row")
+        b2_all = const.tile([P, D], BF16, tag="b2_all", name="b2_all")
+        ident_bf = const.tile([P, P], BF16, tag="ident_bf", name="ident_bf")
         clamped = const.tile([P, 1], F32, tag="clamped", name="clamped")
         logit_scale = const.tile([P, 1], F32, tag="logit_scale", name="logit_scale")
         ident = const.tile([P, P], F32, tag="ident", name="ident")
@@ -260,13 +274,18 @@ def tile_moelayer_kernel(tc, x, W1, b1, W2, b2, temperature, out):
         nc.gpsimd.memset(zero[:], 0.0)
         nc.gpsimd.memset(b1_rows[:], 0.0)
         make_identity(nc, ident[:])
+        nc.gpsimd.memset(temp_row[:], 0.0)
+        nc.gpsimd.memset(b2_all[:], 0.0)
+        make_identity(nc, ident_bf[:])
         for w in range(RAW_BUFS):
             load_matrix(w)
-        nc.scalar.dma_start(out=temp[:], in_=temperature.partition_broadcast(P))
+        nc.scalar.dma_start(out=temp_row[0:1, 0:1], in_=temperature.rearrange("(a b) -> a b", a=1))
         nc.scalar.activation(out=warm[:], in_=zero[:], func=ACT.Exp)
         nc.scalar.dma_start(out=b1_rows[0 : E * UNITS, :], in_=b1.rearrange("e (q c) -> (e q) c", q=UNITS))
+        nc.scalar.dma_start(out=b2_all[0:E, :], in_=b2)
 
         b1_turned = {}
+        temp_wide = {}
         for s in range(-X_TURN, n_units + M2_LAG + 2):
             if unit(s - BANK_LAG)[0] == 1:
                 empty_bank(s - BANK_LAG)
@@ -274,7 +293,7 @@ def tile_moelayer_kernel(tc, x, W1, b1, W2, b2, temperature, out):
             if kind == 1 and q == 0:
                 x_grouped[e] = work.tile([P, P, PACK], BF16, tag="x_grouped", name="x_grouped", bufs=2, align_bytes=64)
                 nc.scalar.copy(out=x_grouped[e][:].bitcast(F32), in_=x_turned[e].rearrange("p u r -> p r u"))
-            if s == 2:
+            if s == 3:
                 nc.scalar.activation(out=logit_scale[:], in_=clamped[:], func=ACT.Exp)
             kind, e, q = unit(s)
             if kind == 2 and q == 0:
@@ -287,8 +306,8 @@ def tile_moelayer_kernel(tc, x, W1, b1, W2, b2, temperature, out):
                 quantize(s)
             if s in batch_steps[1:]:
                 interleave_gpsimd(s + G_AHEAD)
-            if s == 1:
-                nc.vector.tensor_scalar_min(out=clamped[:], in0=temp[:], scalar1=CLAMP_MAX)
+            if s == 2:
+                nc.vector.tensor_scalar_min(out=clamped[:], in0=temp_wide[0][:, 0:1], scalar1=CLAMP_MAX)
             if s == 3:
                 nc.vector.tensor_copy(out=b1_grouped[:].bitcast(F32), in_=b1_turned[0].rearrange("p u r -> p r u"))
             if s in batch_steps:
@@ -309,6 +328,10 @@ def tile_moelayer_kernel(tc, x, W1, b1, W2, b2, temperature, out):
                 x_turned[e] = turn_words(x_rows[e])
             if s == 1:
                 b1_turned[0] = turn_words(b1_rows)
+                temp_wide[0] = spread_row(temp_row, 0, T_COLS)
+            kind, e, q = unit(s + B2_AHEAD)
+            if kind == 2 and q == 0:
+                b2_wide[e] = spread_row(b2_all, e, D)
             if unit(s - BANK_LAG)[0] == 1:
                 turn(s - BANK_LAG)
             if unit(s)[0] == 1:

@@ -271,11 +271,11 @@ def tile_moelayer_kernel(tc, x, W1, b1, W2, b2, temperature, out):
         b1_rows = const.tile([P, D], BF16, tag="b1_rows", name="b1_rows")
         b1_grouped = const.tile([P, P, PACK], BF16, tag="b1_grouped", name="b1_grouped")
 
-        nc.gpsimd.memset(zero[:], 0.0)
-        nc.gpsimd.memset(b1_rows[:], 0.0)
+        nc.vector.memset(zero[:], 0.0)
+        nc.vector.memset(temp_row[:], 0.0)
+        nc.vector.memset(b1_rows[:], 0.0)
+        nc.vector.memset(b2_all[:], 0.0)
         make_identity(nc, ident[:])
-        nc.gpsimd.memset(temp_row[:], 0.0)
-        nc.gpsimd.memset(b2_all[:], 0.0)
         make_identity(nc, ident_bf[:])
         for w in range(RAW_BUFS):
             load_matrix(w)

@@ -38,6 +38,7 @@ EARLY = 3
 BANKS = 7
 T_COLS = 64
 B2_AHEAD = 2
+RUN = 8
 
 
 def tile_moelayer_kernel(tc, x, W1, b1, W2, b2, temperature, out):
@@ -135,8 +136,8 @@ def tile_moelayer_kernel(tc, x, W1, b1, W2, b2, temperature, out):
                 grouped[n] = work.tile([P, N_TILE, PACK], BF16, tag="grouped_g", name="grouped_g", bufs=1, align_bytes=64)
             else:
                 grouped[n] = work.tile([P, N_TILE, PACK], BF16, tag="grouped", name="grouped", bufs=6, align_bytes=64)
-            dst = grouped[n][:, lo:N_TILE, :].rearrange("p (c i) j -> p c j i", i=4)
-            src = raw_unit[n][:, :, lo:N_TILE].rearrange("p j (c i) -> p c j i", i=4)
+            dst = grouped[n][:, lo:N_TILE, :].rearrange("p (c i) j -> p c j i", i=RUN)
+            src = raw_unit[n][:, :, lo:N_TILE].rearrange("p j (c i) -> p c j i", i=RUN)
             if on_scalar(n):
                 nc.scalar.copy(out=dst, in_=src)
             else:

@@ -39,6 +39,7 @@ BANKS = 7
 T_COLS = 64
 B2_AHEAD = 2
 RUN = 8
+PART_LAG = 3
 
 
 def tile_moelayer_kernel(tc, x, W1, b1, W2, b2, temperature, out):
@@ -57,10 +58,13 @@ def tile_moelayer_kernel(tc, x, W1, b1, W2, b2, temperature, out):
     first = [stream.index((1, e, 0)) for e in range(E)]
     batch_steps = [first[e] + BATCH_LAG for e in range(E)]
     finish_step = {}
-    for e in range(E):
+    for e in range(E - 1):
         ready = stream.index((2, e, UNITS - 1)) + M2_LAG + 1
         later = [b for b in batch_steps if b >= ready]
         finish_step[e] = min(later) if later else ready
+
+    def by_columns(n):
+        return n >= n_units - UNITS
 
     def on_scalar(n):
         return ((n + 1) * SCALAR_UNITS) // n_units > (n * SCALAR_UNITS) // n_units
@@ -88,6 +92,8 @@ def tile_moelayer_kernel(tc, x, W1, b1, W2, b2, temperature, out):
         h_codes = {}
         h_scales = {}
         acc = {}
+        acc_part = {}
+        res_last = {}
         b2_wide = {}
         b2_scaled = {}
 
@@ -115,13 +121,22 @@ def tile_moelayer_kernel(tc, x, W1, b1, W2, b2, temperature, out):
                     rows = slice(c * width, (c + 1) * width)
                     nc.sync.dma_start(out=raw[:, rows], in_=src[:, rows])
                 for q in range(UNITS):
-                    raw_unit[UNITS * w + q] = raw[:, q]
+                    if e == E - 1:
+                        raw_unit[UNITS * w + q] = raw[:, :, :, q * P : (q + 1) * P]
+                    else:
+                        raw_unit[UNITS * w + q] = raw[:, q]
 
         def interleave_gpsimd(n):
             grouped[n] = work.tile([P, N_TILE, PACK], BF16, tag="grouped_g", name="grouped_g", bufs=1, align_bytes=64)
+            if by_columns(n):
+                dst = grouped[n][:, 0:G_COLS, :].rearrange("p (g c) j -> p g c j", c=P)
+                src = raw_unit[n][:, 0 : G_COLS // P].rearrange("p g j c -> p g c j")
+            else:
+                dst = grouped[n][:, 0:G_COLS, :]
+                src = raw_unit[n][:, :, 0:G_COLS].rearrange("p j c -> p c j")
             nc.gpsimd.tensor_scalar(
-                out=grouped[n][:, 0:G_COLS, :],
-                in0=raw_unit[n][:, :, 0:G_COLS].rearrange("p j c -> p c j"),
+                out=dst,
+                in0=src,
                 scalar1=1.0,
                 scalar2=0.0,
                 op0=ALU.mult,
@@ -136,8 +151,12 @@ def tile_moelayer_kernel(tc, x, W1, b1, W2, b2, temperature, out):
                 grouped[n] = work.tile([P, N_TILE, PACK], BF16, tag="grouped_g", name="grouped_g", bufs=1, align_bytes=64)
             else:
                 grouped[n] = work.tile([P, N_TILE, PACK], BF16, tag="grouped", name="grouped", bufs=6, align_bytes=64)
-            dst = grouped[n][:, lo:N_TILE, :].rearrange("p (c i) j -> p c j i", i=RUN)
-            src = raw_unit[n][:, :, lo:N_TILE].rearrange("p j (c i) -> p c j i", i=RUN)
+            if by_columns(n):
+                dst = grouped[n][:, lo:N_TILE, :].rearrange("p (g c i) j -> p g c j i", c=P // RUN, i=RUN)
+                src = raw_unit[n][:, lo // P : UNITS].rearrange("p g j (c i) -> p g c j i", i=RUN)
+            else:
+                dst = grouped[n][:, lo:N_TILE, :].rearrange("p (c i) j -> p c j i", i=RUN)
+                src = raw_unit[n][:, :, lo:N_TILE].rearrange("p j (c i) -> p c j i", i=RUN)
             if on_scalar(n):
                 nc.scalar.copy(out=dst, in_=src)
             else:
@@ -165,6 +184,18 @@ def tile_moelayer_kernel(tc, x, W1, b1, W2, b2, temperature, out):
                     start=True,
                     stop=True,
                 )
+            elif by_columns(n):
+                acc_part[q] = psum.tile([P, P], F32, tag="bank", name="acc_part", bufs=BANKS)
+                for g in range(UNITS):
+                    nc.tensor.matmul_mx(
+                        out=acc_part[q][:],
+                        lhsT=h_codes[e][:, g, :].bitcast(FP8X4),
+                        lhsT_scale=h_scales[e][:, g, :],
+                        rhs=codes[n][:, g * P : (g + 1) * P].bitcast(FP8X4),
+                        rhs_scale=scales[n][:, g * P : (g + 1) * P],
+                        start=(g == 0),
+                        stop=(g == UNITS - 1),
+                    )
             else:
                 if q == 0:
                     acc[e] = psum.tile([P, D], F32, tag="bank", name="acc", bufs=BANKS)
@@ -245,6 +276,24 @@ def tile_moelayer_kernel(tc, x, W1, b1, W2, b2, temperature, out):
             )
             nc.sync.dma_start(out=out[e * P : (e + 1) * P, :], in_=res[:])
 
+        def finish_part(q):
+            e = E - 1
+            cols = slice(q * P, (q + 1) * P)
+            if q == 0:
+                res_last[0] = work.tile([P, D], F32, tag="res", name="res_last", bufs=2)
+            res = res_last[0]
+            nc.vector.scalar_tensor_tensor(
+                out=res[:, cols],
+                in0=acc_part[q][:],
+                scalar=logit_scale[:, 0:1],
+                in1=b2_scaled[e][:, cols],
+                op0=ALU.mult,
+                op1=ALU.add,
+            )
+            if q >= UNITS - 2:
+                done = slice(0, (q + 1) * P) if q == UNITS - 2 else cols
+                nc.sync.dma_start(out=out[e * P : (e + 1) * P, done], in_=res[:, done])
+
         def turn_words(rows):
             words = rows[:].bitcast(F32)
             t = psum.tile([P, 2, P], F32, tag="bank", name="words", bufs=BANKS)
@@ -303,6 +352,8 @@ def tile_moelayer_kernel(tc, x, W1, b1, W2, b2, temperature, out):
                 interleave(s + SCALAR_LEAD)
             if unit(s + VECTOR_LEAD)[0] and not on_scalar(s + VECTOR_LEAD):
                 interleave(s + VECTOR_LEAD)
+            if by_columns(s - PART_LAG) and s - PART_LAG < n_units:
+                finish_part(s - PART_LAG - (n_units - UNITS))
             if unit(s)[0]:
                 quantize(s)
             if s in batch_steps[1:]:
@@ -314,7 +365,7 @@ def tile_moelayer_kernel(tc, x, W1, b1, W2, b2, temperature, out):
             if s in batch_steps:
                 for q in range(0, UNITS, 2):
                     add_bias(s - BATCH_LAG + q)
-            for e in range(E):
+            for e in range(E - 1):
                 if finish_step[e] == s:
                     finish(e)
             if s - 1 in batch_steps:

@@ -40,6 +40,9 @@ T_COLS = 64
 B2_AHEAD = 2
 RUN = 8
 PART_LAG = 3
+PASS_EXPERTS = (4, 5, 6, 7)
+PASS_UNIT = 2
+PASS_LEAD = 5
 
 
 def tile_moelayer_kernel(tc, x, W1, b1, W2, b2, temperature, out):
@@ -66,8 +69,10 @@ def tile_moelayer_kernel(tc, x, W1, b1, W2, b2, temperature, out):
     def by_columns(n):
         return n >= n_units - UNITS
 
+    pass_units = [first[e] + PASS_UNIT for e in PASS_EXPERTS]
+
     def on_scalar(n):
-        return ((n + 1) * SCALAR_UNITS) // n_units > (n * SCALAR_UNITS) // n_units
+        return n in pass_units or ((n + 1) * SCALAR_UNITS) // n_units > (n * SCALAR_UNITS) // n_units
 
     with ExitStack() as ctx:
         const = ctx.enter_context(tc.tile_pool(name="const", bufs=1))
@@ -96,6 +101,7 @@ def tile_moelayer_kernel(tc, x, W1, b1, W2, b2, temperature, out):
         res_last = {}
         b2_wide = {}
         b2_scaled = {}
+        passed = {}
 
         def load_matrix(w):
             kind, e, q0 = stream[UNITS * w]
@@ -143,7 +149,31 @@ def tile_moelayer_kernel(tc, x, W1, b1, W2, b2, temperature, out):
                 op1=ALU.add,
             )
 
+        def pass_through(n):
+            for half in range(2):
+                passed[(n, half)] = psum.tile([P, 2 * N_TILE], BF16, tag="bank", name="passed", bufs=BANKS)
+                for c in range(2):
+                    first_col = (2 * half + c) * P
+                    nc.tensor.matmul(
+                        out=passed[(n, half)][:, c * N_TILE : (c + 1) * N_TILE].rearrange("p (c j) -> p c j", j=PACK),
+                        lhsT=ident_bf[:],
+                        rhs=raw_unit[n][:, :, first_col : first_col + P].rearrange("p j c -> p c j"),
+                        start=True,
+                        stop=True,
+                    )
+
+        def empty_passed(n):
+            grouped[n] = work.tile([P, N_TILE, PACK], BF16, tag="grouped", name="grouped", bufs=6, align_bytes=64)
+            for half in range(2):
+                nc.scalar.copy(
+                    out=grouped[n][:, half * (N_TILE // 2) : (half + 1) * (N_TILE // 2), :].rearrange("p c j -> p (c j)"),
+                    in_=passed[(n, half)][:],
+                )
+
         def interleave(n):
+            if n in pass_units:
+                empty_passed(n)
+                return
             lo = 0
             if n in grouped:
                 lo = G_COLS
@@ -375,6 +405,8 @@ def tile_moelayer_kernel(tc, x, W1, b1, W2, b2, temperature, out):
             kind, e, q = unit(s + X_QUANT)
             if kind == 1 and q == 0:
                 quantize_x(e)
+            if s + PASS_LEAD in pass_units:
+                pass_through(s + PASS_LEAD)
             kind, e, q = unit(s + X_TURN)
             if kind == 1 and q == 0:
                 x_turned[e] = turn_words(x_rows[e])

@@ -42,7 +42,7 @@ RUN = 8
 PART_LAG = 3
 PASS_EXPERTS = (4, 5, 6, 7)
 PASS_UNIT = 2
-PASS_LEAD = 5
+PASS_LEAD = 6
 
 
 def tile_moelayer_kernel(tc, x, W1, b1, W2, b2, temperature, out):
@@ -155,9 +155,9 @@ def tile_moelayer_kernel(tc, x, W1, b1, W2, b2, temperature, out):
                 for c in range(2):
                     first_col = (2 * half + c) * P
                     nc.tensor.matmul(
-                        out=passed[(n, half)][:, c * N_TILE : (c + 1) * N_TILE].rearrange("p (c j) -> p c j", j=PACK),
+                        out=passed[(n, half)][:, c * N_TILE : (c + 1) * N_TILE].rearrange("p (b i j) -> p b j i", i=RUN, j=PACK),
                         lhsT=ident_bf[:],
-                        rhs=raw_unit[n][:, :, first_col : first_col + P].rearrange("p j c -> p c j"),
+                        rhs=raw_unit[n][:, :, first_col : first_col + P].rearrange("p j (b i) -> p b j i", i=RUN),
                         start=True,
                         stop=True,
                     )

@@ -40,8 +40,7 @@ T_COLS = 64
 B2_AHEAD = 2
 RUN = 8
 PART_LAG = 3
-PASS_EXPERTS = (4, 5, 6, 7)
-PASS_UNIT = 2
+PASS_PLACES = ((4, 2), (5, 2), (6, 2), (6, 5), (7, 2), (7, 5))
 PASS_LEAD = 6
 
 
@@ -69,7 +68,7 @@ def tile_moelayer_kernel(tc, x, W1, b1, W2, b2, temperature, out):
     def by_columns(n):
         return n >= n_units - UNITS
 
-    pass_units = [first[e] + PASS_UNIT for e in PASS_EXPERTS]
+    pass_units = [first[e] + place for e, place in PASS_PLACES]
 
     def on_scalar(n):
         return n in pass_units or ((n + 1) * SCALAR_UNITS) // n_units > (n * SCALAR_UNITS) // n_units
@@ -290,9 +289,16 @@ def tile_moelayer_kernel(tc, x, W1, b1, W2, b2, temperature, out):
             )
             return t
 
+        def spread_b2(e):
+            t = psum.tile([P, D], F32, tag="spread", name="spread", bufs=1)
+            for c in range(UNITS):
+                col = UNITS * e + c
+                nc.tensor.transpose(out=t[:, c * P : (c + 1) * P], in_=b2_cols[:, col : col + 1].to_broadcast([P, P]), identity=ident[:])
+            return t
+
         def scale_b2(e):
             b2_scaled[e] = work.tile([P, D], F32, tag="b2_scaled", name="b2_scaled", bufs=2)
-            nc.scalar.activation(out=b2_scaled[e][:], in_=b2_wide[e][:], func=ACT.Copy, scale=logit_scale[:, 0:1])
+            nc.scalar.copy(out=b2_scaled[e][:], in_=b2_wide[e][:])
 
         def finish(e):
             res = work.tile([P, D], F32, tag="res", name="res", bufs=2)
@@ -343,7 +349,8 @@ def tile_moelayer_kernel(tc, x, W1, b1, W2, b2, temperature, out):
         zero = const.tile([P, 1], F32, tag="zero", name="zero")
         warm = const.tile([P, 1], F32, tag="warm", name="warm")
         temp_row = const.tile([P, T_COLS], BF16, tag="temp_row", name="temp_row")
-        b2_all = const.tile([P, D], BF16, tag="b2_all", name="b2_all")
+        b2_rows = const.tile([P, P], BF16, tag="b2_rows", name="b2_rows")
+        b2_cols = const.tile([P, P], F32, tag="b2_cols", name="b2_cols")
         ident_bf = const.tile([P, P], BF16, tag="ident_bf", name="ident_bf")
         clamped = const.tile([P, 1], F32, tag="clamped", name="clamped")
         logit_scale = const.tile([P, 1], F32, tag="logit_scale", name="logit_scale")
@@ -354,7 +361,7 @@ def tile_moelayer_kernel(tc, x, W1, b1, W2, b2, temperature, out):
         nc.vector.memset(zero[:], 0.0)
         nc.vector.memset(temp_row[:], 0.0)
         nc.vector.memset(b1_rows[:], 0.0)
-        nc.vector.memset(b2_all[:], 0.0)
+        nc.vector.memset(b2_rows[:], 0.0)
         make_identity(nc, ident[:])
         make_identity(nc, ident_bf[:])
         for w in range(RAW_BUFS):
@@ -362,10 +369,11 @@ def tile_moelayer_kernel(tc, x, W1, b1, W2, b2, temperature, out):
         nc.scalar.dma_start(out=temp_row[0:1, 0:1], in_=temperature.rearrange("(a b) -> a b", a=1))
         nc.scalar.activation(out=warm[:], in_=zero[:], func=ACT.Exp)
         nc.scalar.dma_start(out=b1_rows[0 : E * UNITS, :], in_=b1.rearrange("e (q c) -> (e q) c", q=UNITS))
-        nc.scalar.dma_start(out=b2_all[0:E, :], in_=b2)
+        nc.scalar.dma_start(out=b2_rows[0 : E * UNITS, :], in_=b2.rearrange("e (c n) -> (e c) n", n=P))
 
         b1_turned = {}
         temp_wide = {}
+        b2_turned = {}
         for s in range(-X_TURN, n_units + M2_LAG + 2):
             if unit(s - BANK_LAG)[0] == 1:
                 empty_bank(s - BANK_LAG)
@@ -375,6 +383,7 @@ def tile_moelayer_kernel(tc, x, W1, b1, W2, b2, temperature, out):
                 nc.scalar.copy(out=x_grouped[e][:].bitcast(F32), in_=x_turned[e].rearrange("p u r -> p r u"))
             if s == 3:
                 nc.scalar.activation(out=logit_scale[:], in_=clamped[:], func=ACT.Exp)
+                nc.scalar.activation(out=b2_cols[:], in_=b2_turned[0][:], func=ACT.Copy, scale=logit_scale[:, 0:1])
             kind, e, q = unit(s)
             if kind == 2 and q == 0:
                 scale_b2(e)
@@ -413,9 +422,11 @@ def tile_moelayer_kernel(tc, x, W1, b1, W2, b2, temperature, out):
             if s == 1:
                 b1_turned[0] = turn_words(b1_rows)
                 temp_wide[0] = spread_row(temp_row, 0, T_COLS)
+                b2_turned[0] = psum.tile([P, P], BF16, tag="bank", name="b2_turned", bufs=BANKS)
+                nc.tensor.transpose(out=b2_turned[0][:], in_=b2_rows[:], identity=ident_bf[:])
             kind, e, q = unit(s + B2_AHEAD)
             if kind == 2 and q == 0:
-                b2_wide[e] = spread_row(b2_all, e, D)
+                b2_wide[e] = spread_b2(e)
             if unit(s - BANK_LAG)[0] == 1:
                 turn(s - BANK_LAG)
             if unit(s)[0] == 1:

@@ -42,6 +42,7 @@ RUN = 8
 PART_LAG = 3
 PASS_PLACES = ((4, 2), (5, 2), (6, 2), (6, 5), (7, 2), (7, 5))
 PASS_LEAD = 6
+TO_VECTOR = ((6, 3),)
 
 
 def tile_moelayer_kernel(tc, x, W1, b1, W2, b2, temperature, out):
@@ -70,7 +71,11 @@ def tile_moelayer_kernel(tc, x, W1, b1, W2, b2, temperature, out):
 
     pass_units = [first[e] + place for e, place in PASS_PLACES]
 
+    to_vector = [first[e] + place for e, place in TO_VECTOR]
+
     def on_scalar(n):
+        if n in to_vector:
+            return False
         return n in pass_units or ((n + 1) * SCALAR_UNITS) // n_units > (n * SCALAR_UNITS) // n_units
 
     with ExitStack() as ctx:

@@ -42,6 +42,7 @@ RUN = 8
 PART_LAG = 3
 PASS_PLACES = ((4, 2), (5, 2), (6, 2), (6, 5), (7, 2), (7, 5))
 PASS_LEAD = 6
+RES_BUFS = 4
 TO_VECTOR = ((6, 3),)
 
 
@@ -306,7 +307,7 @@ def tile_moelayer_kernel(tc, x, W1, b1, W2, b2, temperature, out):
             nc.scalar.copy(out=b2_scaled[e][:], in_=b2_wide[e][:])
 
         def finish(e):
-            res = work.tile([P, D], F32, tag="res", name="res", bufs=2)
+            res = work.tile([P, D], F32, tag="res", name="res", bufs=RES_BUFS)
             nc.vector.scalar_tensor_tensor(
                 out=res[:],
                 in0=acc[e][:],
@@ -321,7 +322,7 @@ def tile_moelayer_kernel(tc, x, W1, b1, W2, b2, temperature, out):
             e = E - 1
             cols = slice(q * P, (q + 1) * P)
             if q == 0:
-                res_last[0] = work.tile([P, D], F32, tag="res", name="res_last", bufs=2)
+                res_last[0] = work.tile([P, D], F32, tag="res", name="res_last", bufs=RES_BUFS)
             res = res_last[0]
             nc.vector.scalar_tensor_tensor(
                 out=res[:, cols],

from contextlib import ExitStack
import math

import concourse.mybir as mybir
from concourse.masks import make_identity

N_TOK, D, H, E = 1024, 512, 2048, 8
FLOPS = 4 * N_TOK * D * H

F32 = mybir.dt.float32
BF16 = mybir.dt.bfloat16
U32 = mybir.dt.uint32
U8 = mybir.dt.uint8
FP8X4 = mybir.dt.float8_e4m3fn_x4
ALU = mybir.AluOpType
ACT = mybir.ActivationFunctionType

P = 128
PACK = 4
N_TILE = 512
UNITS = 4
CLAMP_MAX = math.log(100.0)

RAW_BUFS = 7
SCALAR_UNITS = 35
SCALAR_LEAD = 3
VECTOR_LEAD = 1
X_TURN = 6
X_COPY = 4
X_QUANT = 1
BANK_LAG = 2
BIAS_LAG = 4
M2_LAG = 2
G_COLS = 256
BATCH_LAG = 7
G_AHEAD = 4
EARLY = 3
BANKS = 7
T_COLS = 64
B2_AHEAD = 2
RUN = 8
PART_LAG = 3
PASS_PLACES = ((4, 2), (5, 2), (6, 2), (6, 5), (7, 2), (7, 5))
PASS_LEAD = 6
RES_BUFS = 4
TO_VECTOR = ((6, 3),)


def tile_moelayer_kernel(tc, x, W1, b1, W2, b2, temperature, out):
    nc = tc.nc

    stream = [(1, 0, q) for q in range(UNITS)]
    for e in range(1, E):
        stream.extend([(1, e, q) for q in range(UNITS)])
        stream.extend([(2, e - 1, q) for q in range(UNITS)])
    stream.extend([(2, E - 1, q) for q in range(UNITS)])
    n_units = len(stream)

    def unit(n):
        return stream[n] if 0 <= n < n_units else (0, 0, 0)

    first = [stream.index((1, e, 0)) for e in range(E)]
    batch_steps = [first[e] + BATCH_LAG for e in range(E)]
    finish_step = {}
    for e in range(E - 1):
        ready = stream.index((2, e, UNITS - 1)) + M2_LAG + 1
        later = [b for b in batch_steps if b >= ready]
        finish_step[e] = min(later) if later else ready

    def by_columns(n):
        return n >= n_units - UNITS

    pass_units = [first[e] + place for e, place in PASS_PLACES]

    to_vector = [first[e] + place for e, place in TO_VECTOR]

    def on_scalar(n):
        if n in to_vector:
            return False
        return n in pass_units or ((n + 1) * SCALAR_UNITS) // n_units > (n * SCALAR_UNITS) // n_units

    with ExitStack() as ctx:
        const = ctx.enter_context(tc.tile_pool(name="const", bufs=1))
        work = ctx.enter_context(tc.tile_pool(name="work", bufs=2))
        psum = ctx.enter_context(tc.psum_pool(name="psum", bufs=8))
        ctx.enter_context(tc.manual_schedule())

        raw_unit = {}
        grouped = {}
        codes = {}
        scales = {}
        bank = {}
        turned = {}
        h_rows = {}
        x_rows = {}
        x_turned = {}
        x_grouped = {}
        x_codes = {}
        x_scales = {}
        h_biased = {}
        h_relu = {}
        h_codes = {}
        h_scales = {}
        acc = {}
        acc_part = {}
        res_last = {}
        b2_wide = {}
        b2_scaled = {}
        passed = {}

        def load_matrix(w):
            kind, e, q0 = stream[UNITS * w]
            if kind == 1:
                x_rows[e] = work.tile([P, D], BF16, tag="x_rows", name="x_rows", bufs=E)
                queue = nc.scalar if w < 2 else nc.sync
                queue.dma_start(out=x_rows[e][:], in_=x[e * P : (e + 1) * P, :])
                raw = work.tile([P, PACK, H], BF16, tag="raw", name="raw", bufs=RAW_BUFS)
                src = W1[e].rearrange("(p j) h -> p j h", j=PACK)
                pieces = UNITS if w < EARLY else 1
                width = H // pieces
                for c in range(pieces):
                    cols = slice(c * width, (c + 1) * width)
                    nc.sync.dma_start(out=raw[:, :, cols], in_=src[:, :, cols])
                for q in range(UNITS):
                    raw_unit[UNITS * w + q] = raw[:, :, q * N_TILE : (q + 1) * N_TILE]
            else:
                raw = work.tile([P, UNITS, PACK, D], BF16, tag="raw", name="raw", bufs=RAW_BUFS)
                src = W2[e].rearrange("(g p j) d -> p g j d", g=UNITS, j=PACK)
                pieces = UNITS if w < EARLY else 1
                width = UNITS // pieces
                for c in range(pieces):
                    rows = slice(c * width, (c + 1) * width)
                    nc.sync.dma_start(out=raw[:, rows], in_=src[:, rows])
                for q in range(UNITS):
                    if e == E - 1:
                        raw_unit[UNITS * w + q] = raw[:, :, :, q * P : (q + 1) * P]
                    else:
                        raw_unit[UNITS * w + q] = raw[:, q]

        def interleave_gpsimd(n):
            grouped[n] = work.tile([P, N_TILE, PACK], BF16, tag="grouped_g", name="grouped_g", bufs=1, align_bytes=64)
            if by_columns(n):
                dst = grouped[n][:, 0:G_COLS, :].rearrange("p (g c) j -> p g c j", c=P)
                src = raw_unit[n][:, 0 : G_COLS // P].rearrange("p g j c -> p g c j")
            else:
                dst = grouped[n][:, 0:G_COLS, :]
                src = raw_unit[n][:, :, 0:G_COLS].rearrange("p j c -> p c j")
            nc.gpsimd.tensor_scalar(
                out=dst,
                in0=src,
                scalar1=1.0,
                scalar2=0.0,
                op0=ALU.mult,
                op1=ALU.add,
            )

        def pass_through(n):
            for half in range(2):
                passed[(n, half)] = psum.tile([P, 2 * N_TILE], BF16, tag="bank", name="passed", bufs=BANKS)
                for c in range(2):
                    first_col = (2 * half + c) * P
                    nc.tensor.matmul(
                        out=passed[(n, half)][:, c * N_TILE : (c + 1) * N_TILE].rearrange("p (b i j) -> p b j i", i=RUN, j=PACK),
                        lhsT=ident_bf[:],
                        rhs=raw_unit[n][:, :, first_col : first_col + P].rearrange("p j (b i) -> p b j i", i=RUN),
                        start=True,
                        stop=True,
                    )

        def empty_passed(n):
            grouped[n] = work.tile([P, N_TILE, PACK], BF16, tag="grouped", name="grouped", bufs=6, align_bytes=64)
            for half in range(2):
                nc.scalar.copy(
                    out=grouped[n][:, half * (N_TILE // 2) : (half + 1) * (N_TILE // 2), :].rearrange("p c j -> p (c j)"),
                    in_=passed[(n, half)][:],
                )

        def interleave(n):
            if n in pass_units:
                empty_passed(n)
                return
            lo = 0
            if n in grouped:
                lo = G_COLS
            elif n in batch_steps:
                grouped[n] = work.tile([P, N_TILE, PACK], BF16, tag="grouped_g", name="grouped_g", bufs=1, align_bytes=64)
            else:
                grouped[n] = work.tile([P, N_TILE, PACK], BF16, tag="grouped", name="grouped", bufs=6, align_bytes=64)
            if by_columns(n):
                dst = grouped[n][:, lo:N_TILE, :].rearrange("p (g c i) j -> p g c j i", c=P // RUN, i=RUN)
                src = raw_unit[n][:, lo // P : UNITS].rearrange("p g j (c i) -> p g c j i", i=RUN)
            else:
                dst = grouped[n][:, lo:N_TILE, :].rearrange("p (c i) j -> p c j i", i=RUN)
                src = raw_unit[n][:, :, lo:N_TILE].rearrange("p j (c i) -> p c j i", i=RUN)
            if on_scalar(n):
                nc.scalar.copy(out=dst, in_=src)
            else:
                nc.vector.tensor_copy(out=dst, in_=src)

        def quantize(n):
            codes[n] = work.tile([P, N_TILE], U32, tag="codes", name="codes", bufs=6, align_bytes=64)
            scales[n] = work.tile([P, N_TILE], U8, tag="scales", name="scales", bufs=6, align_bytes=64)
            nc.vector.quantize_mx(
                out=codes[n][:].bitcast(FP8X4),
                scales=scales[n][:],
                in_=grouped[n].rearrange("p c j -> p (c j)"),
            )

        def multiply(n):
            kind, e, q = stream[n]
            if kind == 1:
                bank[n] = psum.tile([P, N_TILE], BF16, tag="bank", name="bank", bufs=BANKS)
                nc.tensor.matmul_mx(
                    out=bank[n][:],
                    lhsT=x_codes[e][:].bitcast(FP8X4),
                    lhsT_scale=x_scales[e][:],
                    rhs=codes[n][:].bitcast(FP8X4),
                    rhs_scale=scales[n][:],
                    start=True,
                    stop=True,
                )
            elif by_columns(n):
                acc_part[q] = psum.tile([P, P], F32, tag="bank", name="acc_part", bufs=BANKS)
                for g in range(UNITS):
                    nc.tensor.matmul_mx(
                        out=acc_part[q][:],
                        lhsT=h_codes[e][:, g, :].bitcast(FP8X4),
                        lhsT_scale=h_scales[e][:, g, :],
                        rhs=codes[n][:, g * P : (g + 1) * P].bitcast(FP8X4),
                        rhs_scale=scales[n][:, g * P : (g + 1) * P],
                        start=(g == 0),
                        stop=(g == UNITS - 1),
                    )
            else:
                if q == 0:
                    acc[e] = psum.tile([P, D], F32, tag="bank", name="acc", bufs=BANKS)
                nc.tensor.matmul_mx(
                    out=acc[e][:],
                    lhsT=h_codes[e][:, q, :].bitcast(FP8X4),
                    lhsT_scale=h_scales[e][:, q, :],
                    rhs=codes[n][:].bitcast(FP8X4),
                    rhs_scale=scales[n][:],
                    start=(q == 0),
                    stop=(q == UNITS - 1),
                )

        def empty_bank(n):
            h_rows[n] = work.tile([P, N_TILE], BF16, tag="h_rows", name="h_rows", bufs=3)
            nc.scalar.copy(out=h_rows[n][:], in_=bank[n][:])

        def turn(n):
            if n % 2 == 0:
                turned[n] = psum.tile([P, 2, 2, P], F32, tag="bank", name="turned", bufs=BANKS)
            words = h_rows[n][:].bitcast(F32)
            for u in range(2):
                nc.tensor.transpose(out=turned[n - n % 2][:, u, n % 2, :], in_=words[:, u::2], identity=ident[:])

        def add_bias(n):
            kind, e, q = stream[n]
            if q == 0:
                h_biased[e] = work.tile([P, UNITS, P, PACK], BF16, tag="h_biased", name="h_biased", bufs=2)
            row = UNITS * e + q
            nc.vector.tensor_tensor(
                out=h_biased[e][:, q : q + 2].rearrange("p a r (u w) -> p a r u w", w=2),
                in0=turned[n][:].bitcast(BF16).rearrange("p u a (r w) -> p a r u w", w=2),
                in1=b1_grouped[:, row : row + 2, :].unsqueeze(2).to_broadcast([P, 2, P, PACK]).rearrange("p a r (u w) -> p a r u w", w=2),
                op=ALU.add,
            )

        def relu(e):
            h_relu[e] = work.tile([P, UNITS, P, PACK], BF16, tag="h_relu", name="h_relu", bufs=2, align_bytes=64)
            nc.vector.tensor_scalar_max(
                out=h_relu[e].rearrange("p q r t -> p (q r t)"),
                in0=h_biased[e].rearrange("p q r t -> p (q r t)"),
                scalar1=0.0,
            )

        def quantize_h(e):
            h_codes[e] = work.tile([P, UNITS, P], U32, tag="h_codes", name="h_codes", bufs=2, align_bytes=64)
            h_scales[e] = work.tile([P, UNITS, P], U8, tag="h_scales", name="h_scales", bufs=2, align_bytes=64)
            nc.vector.quantize_mx(
                out=h_codes[e].rearrange("p q r -> p (q r)").bitcast(FP8X4),
                scales=h_scales[e].rearrange("p q r -> p (q r)"),
                in_=h_relu[e].rearrange("p q r t -> p (q r t)"),
            )

        def spread_row(rows, r, width):
            t = psum.tile([P, width], F32, tag="spread", name="spread", bufs=1)
            nc.tensor.matmul(
                out=t[:],
                lhsT=ident_bf[:, r : r + 1].to_broadcast([P, P]),
                rhs=rows[:, 0:width],
                start=True,
                stop=True,
            )
            return t

        def spread_b2(e):
            t = psum.tile([P, D], F32, tag="spread", name="spread", bufs=1)
            for c in range(UNITS):
                col = UNITS * e + c
                nc.tensor.transpose(out=t[:, c * P : (c + 1) * P], in_=b2_cols[:, col : col + 1].to_broadcast([P, P]), identity=ident[:])
            return t

        def scale_b2(e):
            b2_scaled[e] = work.tile([P, D], F32, tag="b2_scaled", name="b2_scaled", bufs=2)
            nc.scalar.copy(out=b2_scaled[e][:], in_=b2_wide[e][:])

        def finish(e):
            res = work.tile([P, D], F32, tag="res", name="res", bufs=RES_BUFS)
            nc.vector.scalar_tensor_tensor(
                out=res[:],
                in0=acc[e][:],
                scalar=logit_scale[:, 0:1],
                in1=b2_scaled[e][:],
                op0=ALU.mult,
                op1=ALU.add,
            )
            nc.sync.dma_start(out=out[e * P : (e + 1) * P, :], in_=res[:])

        def finish_part(q):
            e = E - 1
            cols = slice(q * P, (q + 1) * P)
            if q == 0:
                res_last[0] = work.tile([P, D], F32, tag="res", name="res_last", bufs=RES_BUFS)
            res = res_last[0]
            nc.vector.scalar_tensor_tensor(
                out=res[:, cols],
                in0=acc_part[q][:],
                scalar=logit_scale[:, 0:1],
                in1=b2_scaled[e][:, cols],
                op0=ALU.mult,
                op1=ALU.add,
            )
            if q >= UNITS - 2:
                done = slice(0, (q + 1) * P) if q == UNITS - 2 else cols
                nc.sync.dma_start(out=out[e * P : (e + 1) * P, done], in_=res[:, done])

        def turn_words(rows):
            words = rows[:].bitcast(F32)
            t = psum.tile([P, 2, P], F32, tag="bank", name="words", bufs=BANKS)
            for u in range(2):
                nc.tensor.transpose(out=t[:, u, :], in_=words[:, u::2], identity=ident[:])
            return t

        def quantize_x(e):
            x_codes[e] = work.tile([P, P], U32, tag="x_codes", name="x_codes", bufs=2, align_bytes=64)
            x_scales[e] = work.tile([P, P], U8, tag="x_scales", name="x_scales", bufs=2, align_bytes=64)
            nc.vector.quantize_mx(
                out=x_codes[e][:].bitcast(FP8X4),
                scales=x_scales[e][:],
                in_=x_grouped[e].rearrange("p r t -> p (r t)"),
            )

        zero = const.tile([P, 1], F32, tag="zero", name="zero")
        warm = const.tile([P, 1], F32, tag="warm", name="warm")
        temp_row = const.tile([P, T_COLS], BF16, tag="temp_row", name="temp_row")
        b2_rows = const.tile([P, P], BF16, tag="b2_rows", name="b2_rows")
        b2_cols = const.tile([P, P], F32, tag="b2_cols", name="b2_cols")
        ident_bf = const.tile([P, P], BF16, tag="ident_bf", name="ident_bf")
        clamped = const.tile([P, 1], F32, tag="clamped", name="clamped")
        logit_scale = const.tile([P, 1], F32, tag="logit_scale", name="logit_scale")
        ident = const.tile([P, P], F32, tag="ident", name="ident")
        b1_rows = const.tile([P, D], BF16, tag="b1_rows", name="b1_rows")
        b1_grouped = const.tile([P, P, PACK], BF16, tag="b1_grouped", name="b1_grouped")

        nc.vector.memset(zero[:], 0.0)
        nc.vector.memset(temp_row[:], 0.0)
        nc.vector.memset(b1_rows[:], 0.0)
        nc.vector.memset(b2_rows[:], 0.0)
        make_identity(nc, ident[:])
        make_identity(nc, ident_bf[:])
        for w in range(RAW_BUFS):
            load_matrix(w)
        nc.scalar.dma_start(out=temp_row[0:1, 0:1], in_=temperature.rearrange("(a b) -> a b", a=1))
        nc.scalar.activation(out=warm[:], in_=zero[:], func=ACT.Exp)
        nc.scalar.dma_start(out=b1_rows[0 : E * UNITS, :], in_=b1.rearrange("e (q c) -> (e q) c", q=UNITS))
        nc.scalar.dma_start(out=b2_rows[0 : E * UNITS, :], in_=b2.rearrange("e (c n) -> (e c) n", n=P))

        b1_turned = {}
        temp_wide = {}
        b2_turned = {}
        for s in range(-X_TURN, n_units + M2_LAG + 2):
            if unit(s - BANK_LAG)[0] == 1:
                empty_bank(s - BANK_LAG)
            kind, e, q = unit(s + X_COPY)
            if kind == 1 and q == 0:
                x_grouped[e] = work.tile([P, P, PACK], BF16, tag="x_grouped", name="x_grouped", bufs=2, align_bytes=64)
                nc.scalar.copy(out=x_grouped[e][:].bitcast(F32), in_=x_turned[e].rearrange("p u r -> p r u"))
            if s == 3:
                nc.scalar.activation(out=logit_scale[:], in_=clamped[:], func=ACT.Exp)
                nc.scalar.activation(out=b2_cols[:], in_=b2_turned[0][:], func=ACT.Copy, scale=logit_scale[:, 0:1])
            kind, e, q = unit(s)
            if kind == 2 and q == 0:
                scale_b2(e)
            if unit(s + SCALAR_LEAD)[0] and on_scalar(s + SCALAR_LEAD):
                interleave(s + SCALAR_LEAD)
            if unit(s + VECTOR_LEAD)[0] and not on_scalar(s + VECTOR_LEAD):
                interleave(s + VECTOR_LEAD)
            if by_columns(s - PART_LAG) and s - PART_LAG < n_units:
                finish_part(s - PART_LAG - (n_units - UNITS))
            if unit(s)[0]:
                quantize(s)
            if s in batch_steps[1:]:
                interleave_gpsimd(s + G_AHEAD)
            if s == 2:
                nc.vector.tensor_scalar_min(out=clamped[:], in0=temp_wide[0][:, 0:1], scalar1=CLAMP_MAX)
            if s == 3:
                nc.vector.tensor_copy(out=b1_grouped[:].bitcast(F32), in_=b1_turned[0].rearrange("p u r -> p r u"))
            if s in batch_steps:
                for q in range(0, UNITS, 2):
                    add_bias(s - BATCH_LAG + q)
            for e in range(E - 1):
                if finish_step[e] == s:
                    finish(e)
            if s - 1 in batch_steps:
                relu(batch_steps.index(s - 1))
            if s - 2 in batch_steps:
                quantize_h(batch_steps.index(s - 2))
            kind, e, q = unit(s + X_QUANT)
            if kind == 1 and q == 0:
                quantize_x(e)
            if s + PASS_LEAD in pass_units:
                pass_through(s + PASS_LEAD)
            kind, e, q = unit(s + X_TURN)
            if kind == 1 and q == 0:
                x_turned[e] = turn_words(x_rows[e])
            if s == 1:
                b1_turned[0] = turn_words(b1_rows)
                temp_wide[0] = spread_row(temp_row, 0, T_COLS)
                b2_turned[0] = psum.tile([P, P], BF16, tag="bank", name="b2_turned", bufs=BANKS)
                nc.tensor.transpose(out=b2_turned[0][:], in_=b2_rows[:], identity=ident_bf[:])
            kind, e, q = unit(s + B2_AHEAD)
            if kind == 2 and q == 0:
                b2_wide[e] = spread_b2(e)
            if unit(s - BANK_LAG)[0] == 1:
                turn(s - BANK_LAG)
            if unit(s)[0] == 1:
                multiply(s)
            if unit(s - M2_LAG)[0] == 2:
                multiply(s - M2_LAG)
            if s >= 0 and s % UNITS == UNITS - 1 and s // UNITS + RAW_BUFS < 2 * E:
                load_matrix(s // UNITS + RAW_BUFS)
